import numpy as np
import ml_dtypes


def mxq(x, axis, fmt="e4m3"):
    dtype, down = {"e4m3": (ml_dtypes.float8_e4m3fn, 7), "e5m2": (ml_dtypes.float8_e5m2, 14)}[fmt]
    v = np.moveaxis(np.asarray(x, np.float32).astype(ml_dtypes.bfloat16).astype(np.float64), axis, -1)
    blocks = v.reshape(v.shape[:-1] + (-1, 32))
    amax = np.abs(blocks).max(-1, keepdims=True)
    byte = np.maximum(np.where(amax > 0, np.frexp(amax)[1] - 1 + 127, 0) - down, 1)
    scale = np.exp2(byte - 127.0)
    codes = (blocks / scale).astype(np.float32).astype(dtype).astype(np.float64)
    return np.moveaxis((codes * scale).reshape(v.shape), -1, axis)


BF16 = ml_dtypes.bfloat16


def bf(x):
    return np.asarray(x, np.float32).astype(BF16)


def f64(x):
    return np.asarray(x).astype(np.float64)


B, L, D = 8, 512, 768

EPS = 1e-05


def setup_inputs():
    g = 0.5 + np.random.random_sample((B, L, 1))
    c = 1.8 / (L * np.sqrt(D)) ** (1.0 / 3.0)
    return {"inputs": bf(np.random.standard_normal((B, L, D)) * g * c)}


def reference(inputs):
    x = f64(inputs)
    w = np.sqrt(EPS + np.sum(x * x, axis=-1))
    xw = x * w[..., None]
    return mxq(xw, 1, "e4m3").transpose(0, 2, 1) @ mxq(x, 1, "e4m3")

@@ -1,0 +1,199 @@
+from contextlib import ExitStack
+
+import concourse.mybir as mybir
+
+FLOPS = 2 * 8 * 512 * 768 * 768
+
+BF16 = mybir.dt.bfloat16
+F32 = mybir.dt.float32
+U32 = mybir.dt.uint32
+U8 = mybir.dt.uint8
+FP8X4 = mybir.dt.float8_e4m3fn_x4
+ACT = mybir.ActivationFunctionType
+ALU = mybir.AluOpType
+
+B = 8
+D = 768
+P = 128
+PACK = 4
+EPS = 1e-05
+WIDE = 512
+CH = 256
+UNITS = 3 * B
+AHEAD = 2
+ROWS_OF_STEP = ((0, 1), (2,), (3,))
+
+
+def tile_globalmixture_kernel(tc, inputs, out):
+    nc = tc.nc
+    with ExitStack() as ctx:
+        keep = ctx.enter_context(tc.tile_pool(name="keep", bufs=1))
+        small = ctx.enter_context(tc.tile_pool(name="small", bufs=AHEAD + 2))
+        work = ctx.enter_context(tc.tile_pool(name="work", bufs=3))
+        quant = ctx.enter_context(tc.tile_pool(name="quant", bufs=4))
+        stage = ctx.enter_context(tc.tile_pool(name="stage", bufs=8))
+        psum = ctx.enter_context(tc.psum_pool(name="psum", bufs=1))
+
+        eps_t = keep.tile([P, 1], F32, name="eps_t")
+        nc.vector.memset(eps_t[:], EPS)
+        warm = keep.tile([P, 1], F32, name="warm")
+        nc.scalar.activation(out=warm[:], in_=eps_t[:], func=ACT.Sqrt)
+
+        xs = []
+        for b in range(B):
+            xt = keep.tile([P, PACK, D], BF16, name="x%d" % b)
+            src = inputs[b].rearrange("(p j) d -> p j d", j=PACK)
+            if b == 0:
+                for j in range(PACK):
+                    nc.sync.dma_start(out=xt[:, j, :], in_=src[:, j, :])
+            else:
+                nc.sync.dma_start(out=xt[:], in_=src)
+            xs.append(xt)
+
+        sums = {}
+        norms = {}
+        xgs = {}
+        xops = {}
+        wgs = {}
+        wops = {}
+        accs = {}
+        results = {}
+
+        def square_row(b, j):
+            if b not in sums:
+                ss = small.tile([P, PACK], F32, name="ss")
+                sums[b] = ss
+            junk_s = work.tile([P, D], BF16, name="junk_s")
+            nc.scalar.activation(out=junk_s[:], in_=xs[b][:, j, :], func=ACT.Square, accum_out=sums[b][:, j : j + 1])
+
+        def root(b):
+            w = small.tile([P, PACK], F32, name="w")
+            nc.scalar.activation(out=w[:], in_=sums[b][:], func=ACT.Sqrt, bias=eps_t[:])
+            norms[b] = w
+
+        def regroup(dst, src):
+            nc.vector.tensor_copy(
+                out=dst.rearrange("p (c i) t -> p c t i", i=4),
+                in_=src.rearrange("p t (c i) -> p c t i", i=4),
+            )
+
+        def regroup_x(b, c):
+            if b not in xgs:
+                xg = work.tile([P, D, PACK], BF16, name="xg", align_bytes=64)
+                xgs[b] = xg
+            regroup(xgs[b][:, CH * c : CH * c + CH, :], xs[b][:, :, CH * c : CH * c + CH])
+
+        def quantise_x(b, c):
+            if b not in xops:
+                xc = quant.tile([P, D], U32, name="xc", align_bytes=64)
+                xsc = quant.tile([P, D], U8, name="xsc", align_bytes=64)
+                xops[b] = (xc, xsc)
+            xc, xsc = xops[b]
+            nc.vector.quantize_mx(
+                out=xc[:, CH * c : CH * c + CH].bitcast(FP8X4),
+                scales=xsc[:, CH * c : CH * c + CH],
+                in_=xgs[b][:, CH * c : CH * c + CH, :].rearrange("p w j -> p (w j)"),
+            )
+
+        def weigh(u):
+            b = u // 3
+            c = u % 3
+            xwn = work.tile([P, PACK, CH], BF16, name="xwn")
+            for j in range(PACK):
+                nc.vector.tensor_scalar(
+                    out=xwn[:, j, :], in0=xs[b][:, j, CH * c : CH * c + CH], scalar1=norms[b][:, j : j + 1],
+                    scalar2=None, op0=ALU.mult,
+                )
+            xwg = work.tile([P, CH, PACK], BF16, name="xwg", align_bytes=64)
+            regroup(xwg[:], xwn[:])
+            wgs[u] = xwg
+
+        def quantise_w(u):
+            wc = quant.tile([P, CH], U32, name="wc", align_bytes=64)
+            wsc = quant.tile([P, CH], U8, name="wsc", align_bytes=64)
+            nc.vector.quantize_mx(
+                out=wc[:].bitcast(FP8X4), scales=wsc[:], in_=wgs[u][:].rearrange("p w j -> p (w j)")
+            )
+            wops[u] = (wc, wsc)
+
+        def mx(acc, u, half, lo, hi):
+            xc, xsc = xops[u // 3]
+            wc, wsc = wops[u]
+            nc.tensor.matmul_mx(
+                out=acc,
+                lhsT=wc[:, P * half : P * half + P].bitcast(FP8X4),
+                lhsT_scale=wsc[:, P * half : P * half + P],
+                rhs=xc[:, lo:hi].bitcast(FP8X4),
+                rhs_scale=xsc[:, lo:hi],
+                start=True,
+                stop=True,
+            )
+
+        def multiply(u):
+            for r in range(3):
+                slot = (3 * u + r) % 8
+                if r == 1:
+                    acc = psum.tile([P, 2, CH], F32, name="acc%d" % slot)
+                    mx(acc[:, 0, :], u, 0, WIDE, D)
+                    mx(acc[:, 1, :], u, 1, WIDE, D)
+                else:
+                    acc = psum.tile([P, WIDE], F32, name="acc%d" % slot)
+                    mx(acc[:], u, r // 2, 0, WIDE)
+                accs[(u, r)] = acc
+
+        def on_vector(u, r):
+            helped = u // 3 + AHEAD < B and u % 3 != 0
+            return r == 0 and (helped or u == UNITS - 1)
+
+        def leave(u, r):
+            if u not in results:
+                res = stage.tile([P, 2, D], F32, name="res")
+                results[u] = [res, 0]
+            res = results[u][0]
+            if r == 1:
+                dst = res[:, :, WIDE:D]
+            else:
+                dst = res[:, r // 2, 0:WIDE]
+            if on_vector(u, r):
+                nc.vector.tensor_copy(out=dst, in_=accs[(u, r)][:])
+            else:
+                nc.scalar.copy(out=dst, in_=accs[(u, r)][:])
+            results[u][1] += 1
+            if results[u][1] == 3:
+                out_b = out[u // 3].rearrange("(m p) e -> p m e", p=P)
+                m0 = 2 * (u % 3)
+                nc.sync.dma_start(out=out_b[:, m0 : m0 + 2, :], in_=res[:])
+
+        for b in range(AHEAD):
+            for j in range(PACK):
+                square_row(b, j)
+            root(b)
+        for c in range(3):
+            regroup_x(0, c)
+        for c in range(3):
+            quantise_x(0, c)
+        for u in range(UNITS + 1):
+            b = u // 3
+            c = u % 3
+            if u < UNITS:
+                weigh(u)
+                if b + 1 < B:
+                    regroup_x(b + 1, c)
+            if u > 0:
+                for r in range(3):
+                    if on_vector(u - 1, r):
+                        leave(u - 1, r)
+            if u < UNITS:
+                quantise_w(u)
+                if b + 1 < B:
+                    quantise_x(b + 1, c)
+                multiply(u)
+            if u > 0:
+                for r in range(3):
+                    if not on_vector(u - 1, r):
+                        leave(u - 1, r)
+            if u < UNITS and b + AHEAD < B:
+                for j in ROWS_OF_STEP[c]:
+                    square_row(b + AHEAD, j)
+                if c == 2:
+                    root(b + AHEAD)

@@ -20,19 +20,20 @@ EPS = 1e-05
 WIDE = 512
 CH = 256
 UNITS = 3 * B
-AHEAD = 2
-ROWS_OF_STEP = ((0, 1), (2,), (3,))
+RUN = 4
+LEAD = (-3, -2, -1, -1)
 
 
 def tile_globalmixture_kernel(tc, inputs, out):
     nc = tc.nc
     with ExitStack() as ctx:
         keep = ctx.enter_context(tc.tile_pool(name="keep", bufs=1))
-        small = ctx.enter_context(tc.tile_pool(name="small", bufs=AHEAD + 2))
+        small = ctx.enter_context(tc.tile_pool(name="small", bufs=4))
         work = ctx.enter_context(tc.tile_pool(name="work", bufs=3))
         quant = ctx.enter_context(tc.tile_pool(name="quant", bufs=4))
         stage = ctx.enter_context(tc.tile_pool(name="stage", bufs=8))
         psum = ctx.enter_context(tc.psum_pool(name="psum", bufs=1))
+        ctx.enter_context(tc.manual_schedule())
 
         eps_t = keep.tile([P, 1], F32, name="eps_t")
         nc.vector.memset(eps_t[:], EPS)
@@ -54,17 +55,30 @@ def tile_globalmixture_kernel(tc, inputs, out):
         norms = {}
         xgs = {}
         xops = {}
+        xwns = {}
         wgs = {}
         wops = {}
         accs = {}
         results = {}
 
-        def square_row(b, j):
+        def sums_of(b):
             if b not in sums:
                 ss = small.tile([P, PACK], F32, name="ss")
                 sums[b] = ss
+            return sums[b]
+
+        def square_row(b, j):
+            ss = sums_of(b)
             junk_s = work.tile([P, D], BF16, name="junk_s")
-            nc.scalar.activation(out=junk_s[:], in_=xs[b][:, j, :], func=ACT.Square, accum_out=sums[b][:, j : j + 1])
+            nc.scalar.activation(out=junk_s[:], in_=xs[b][:, j, :], func=ACT.Square, accum_out=ss[:, j : j + 1])
+
+        def square_row_on_vector(b, j):
+            ss = sums_of(b)
+            junk_v = work.tile([P, D], BF16, name="junk_v")
+            nc.vector.scalar_tensor_tensor(
+                out=junk_v[:], in0=xs[b][:, j, :], scalar=1.0, in1=xs[b][:, j, :], op0=ALU.mult, op1=ALU.mult,
+                accum_out=ss[:, j : j + 1],
+            )
 
         def root(b):
             w = small.tile([P, PACK], F32, name="w")
@@ -73,15 +87,14 @@ def tile_globalmixture_kernel(tc, inputs, out):
 
         def regroup(dst, src):
             nc.vector.tensor_copy(
-                out=dst.rearrange("p (c i) t -> p c t i", i=4),
-                in_=src.rearrange("p t (c i) -> p c t i", i=4),
+                out=dst.rearrange("p (c i) t -> p c t i", i=RUN),
+                in_=src.rearrange("p t (c i) -> p c t i", i=RUN),
             )
 
         def regroup_x(b, c):
-            if b not in xgs:
-                xg = work.tile([P, D, PACK], BF16, name="xg", align_bytes=64)
-                xgs[b] = xg
-            regroup(xgs[b][:, CH * c : CH * c + CH, :], xs[b][:, :, CH * c : CH * c + CH])
+            xg = work.tile([P, CH, PACK], BF16, name="xg", align_bytes=64)
+            regroup(xg[:], xs[b][:, :, CH * c : CH * c + CH])
+            xgs[(b, c)] = xg
 
         def quantise_x(b, c):
             if b not in xops:
@@ -92,20 +105,23 @@ def tile_globalmixture_kernel(tc, inputs, out):
             nc.vector.quantize_mx(
                 out=xc[:, CH * c : CH * c + CH].bitcast(FP8X4),
                 scales=xsc[:, CH * c : CH * c + CH],
-                in_=xgs[b][:, CH * c : CH * c + CH, :].rearrange("p w j -> p (w j)"),
+                in_=xgs[(b, c)][:].rearrange("p w j -> p (w j)"),
             )
 
-        def weigh(u):
-            b = u // 3
-            c = u % 3
-            xwn = work.tile([P, PACK, CH], BF16, name="xwn")
+        def weigh(b, lo, hi):
+            if b not in xwns:
+                xwn = work.tile([P, PACK, D], BF16, name="xwn")
+                xwns[b] = xwn
             for j in range(PACK):
                 nc.vector.tensor_scalar(
-                    out=xwn[:, j, :], in0=xs[b][:, j, CH * c : CH * c + CH], scalar1=norms[b][:, j : j + 1],
+                    out=xwns[b][:, j, lo:hi], in0=xs[b][:, j, lo:hi], scalar1=norms[b][:, j : j + 1],
                     scalar2=None, op0=ALU.mult,
                 )
+
+        def regroup_w(u):
+            c = u % 3
             xwg = work.tile([P, CH, PACK], BF16, name="xwg", align_bytes=64)
-            regroup(xwg[:], xwn[:])
+            regroup(xwg[:], xwns[u // 3][:, :, CH * c : CH * c + CH])
             wgs[u] = xwg
 
         def quantise_w(u):
@@ -142,8 +158,11 @@ def tile_globalmixture_kernel(tc, inputs, out):
                 accs[(u, r)] = acc
 
         def on_vector(u, r):
-            helped = u // 3 + AHEAD < B and u % 3 != 0
-            return r == 0 and (helped or u == UNITS - 1)
+            b = u // 3
+            c = u % 3
+            if r == 0:
+                return b == B - 1 or c == 1 or (c == 2 and b < 3)
+            return u == UNITS - 1 and r == 2
 
         def leave(u, r):
             if u not in results:
@@ -151,49 +170,69 @@ def tile_globalmixture_kernel(tc, inputs, out):
                 results[u] = [res, 0]
             res = results[u][0]
             if r == 1:
-                dst = res[:, :, WIDE:D]
+                part = (slice(0, 2), slice(WIDE, D))
             else:
-                dst = res[:, r // 2, 0:WIDE]
+                part = (slice(r // 2, r // 2 + 1), slice(0, WIDE))
+            dst = res[:, part[0], part[1]]
+            src = accs[(u, r)][:] if r == 1 else accs[(u, r)][:].unsqueeze(1)
             if on_vector(u, r):
-                nc.vector.tensor_copy(out=dst, in_=accs[(u, r)][:])
+                nc.vector.tensor_copy(out=dst, in_=src)
             else:
-                nc.scalar.copy(out=dst, in_=accs[(u, r)][:])
+                nc.scalar.copy(out=dst, in_=src)
             results[u][1] += 1
-            if results[u][1] == 3:
-                out_b = out[u // 3].rearrange("(m p) e -> p m e", p=P)
-                m0 = 2 * (u % 3)
+            out_b = out[u // 3].rearrange("(m p) e -> p m e", p=P)
+            m0 = 2 * (u % 3)
+            if u == UNITS - 1:
+                nc.sync.dma_start(out=out_b[:, m0 + part[0].start : m0 + part[0].stop, part[1]], in_=dst)
+            elif results[u][1] == 3:
                 nc.sync.dma_start(out=out_b[:, m0 : m0 + 2, :], in_=res[:])
 
-        for b in range(AHEAD):
+        rows = {}
+        for b in range(1, B):
             for j in range(PACK):
-                square_row(b, j)
-            root(b)
+                rows.setdefault(max(-1, 3 * (b - 1) + LEAD[j]), []).append((b, j))
+
+        square_row_on_vector(0, 0)
+        for j in range(1, PACK):
+            square_row(0, j)
+        root(0)
+        for b, j in rows[-1]:
+            square_row(b, j)
+        root(1)
         for c in range(3):
             regroup_x(0, c)
         for c in range(3):
             quantise_x(0, c)
+        weigh(0, 0, CH)
         for u in range(UNITS + 1):
             b = u // 3
             c = u % 3
             if u < UNITS:
-                weigh(u)
                 if b + 1 < B:
                     regroup_x(b + 1, c)
+                regroup_w(u)
+                if b + 1 < B:
+                    quantise_x(b + 1, c)
+                if b == 0 and c < 2:
+                    weigh(0, CH * (c + 1), CH * (c + 2))
+                if c == 2 and b + 1 < B:
+                    weigh(b + 1, 0, D)
             if u > 0:
                 for r in range(3):
                     if on_vector(u - 1, r):
                         leave(u - 1, r)
             if u < UNITS:
                 quantise_w(u)
-                if b + 1 < B:
-                    quantise_x(b + 1, c)
                 multiply(u)
+            ended = []
+            for bb, j in rows.get(u, []):
+                square_row(bb, j)
+                if j == PACK - 1:
+                    ended.append(bb)
             if u > 0:
                 for r in range(3):
                     if not on_vector(u - 1, r):
                         leave(u - 1, r)
-            if u < UNITS and b + AHEAD < B:
-                for j in ROWS_OF_STEP[c]:
-                    square_row(b + AHEAD, j)
-                if c == 2:
-                    root(b + AHEAD)
+                        for bb in ended:
+                            root(bb)
+                        ended = []

@@ -1,6 +1,7 @@
 from contextlib import ExitStack
 
 import concourse.mybir as mybir
+from concourse.masks import make_identity
 
 FLOPS = 2 * 8 * 512 * 768 * 768
 
@@ -21,7 +22,10 @@ WIDE = 512
 CH = 256
 UNITS = 3 * B
 RUN = 4
-LEAD = (-3, -2, -1, -1)
+WORDS = D // 2
+PE_FROM = 2
+PE_ROWS = 3
+BANKS = 6
 
 
 def tile_globalmixture_kernel(tc, inputs, out):
@@ -39,6 +43,9 @@ def tile_globalmixture_kernel(tc, inputs, out):
         nc.vector.memset(eps_t[:], EPS)
         warm = keep.tile([P, 1], F32, name="warm")
         nc.scalar.activation(out=warm[:], in_=eps_t[:], func=ACT.Sqrt)
+
+        ident = keep.tile([P, P], F32, name="ident")
+        make_identity(nc, ident[:])
 
         xs = []
         for b in range(B):
@@ -59,6 +66,8 @@ def tile_globalmixture_kernel(tc, inputs, out):
         wgs = {}
         wops = {}
         accs = {}
+        turned = {}
+        xts = {}
         results = {}
 
         def sums_of(b):
@@ -84,6 +93,36 @@ def tile_globalmixture_kernel(tc, inputs, out):
             w = small.tile([P, PACK], F32, name="w")
             nc.scalar.activation(out=w[:], in_=sums[b][:], func=ACT.Sqrt, bias=eps_t[:])
             norms[b] = w
+
+        def turn(n, b, j):
+            sqt = psum.tile([P, WIDE], F32, name="sqt%d" % (n % 2))
+            words = xs[b][:, j, :].bitcast(F32)
+            for k in range(3):
+                nc.tensor.transpose(sqt[:, P * k : P * k + P], words[:, P * k : P * k + P], ident[:])
+            turned[(b, j)] = sqt
+
+        def turned_out(b, j):
+            xt = work.tile([P, WORDS], F32, name="xt")
+            nc.scalar.copy(out=xt[:], in_=turned[(b, j)][:, 0:WORDS])
+            xts[(b, j)] = xt
+
+        def gram(b, j):
+            halves = xts[(b, j)][:].bitcast(BF16)
+            for k in range(3):
+                for e in range(2):
+                    cols = halves[:, 2 * P * k + e : 2 * P * (k + 1) : 2]
+                    nc.tensor.matmul(
+                        turned[(b, j)][:, WORDS:WIDE], lhsT=cols, rhs=cols, start=(k == 0 and e == 0),
+                        stop=(k == 2 and e == 1),
+                    )
+
+        def diagonal(b, j):
+            ss = sums_of(b)
+            junk_d = work.tile([P, P], F32, name="junk_d")
+            nc.vector.scalar_tensor_tensor(
+                out=junk_d[:], in0=turned[(b, j)][:, WORDS:WIDE], scalar=1.0, in1=ident[:], op0=ALU.mult,
+                op1=ALU.mult, accum_out=ss[:, j : j + 1],
+            )
 
         def regroup(dst, src):
             nc.vector.tensor_copy(
@@ -147,7 +186,7 @@ def tile_globalmixture_kernel(tc, inputs, out):
 
         def multiply(u):
             for r in range(3):
-                slot = (3 * u + r) % 8
+                slot = (3 * u + r) % BANKS
                 if r == 1:
                     acc = psum.tile([P, 2, CH], F32, name="acc%d" % slot)
                     mx(acc[:, 0, :], u, 0, WIDE, D)
@@ -158,11 +197,7 @@ def tile_globalmixture_kernel(tc, inputs, out):
                 accs[(u, r)] = acc
 
         def on_vector(u, r):
-            b = u // 3
-            c = u % 3
-            if r == 0:
-                return b == B - 1 or c == 1 or (c == 2 and b < 3)
-            return u == UNITS - 1 and r == 2
+            return (r == 0 and u >= 3 * (B - 1)) or (r == 2 and u == UNITS - 1)
 
         def leave(u, r):
             if u not in results:
@@ -187,52 +222,63 @@ def tile_globalmixture_kernel(tc, inputs, out):
             elif results[u][1] == 3:
                 nc.sync.dma_start(out=out_b[:, m0 : m0 + 2, :], in_=res[:])
 
-        rows = {}
-        for b in range(1, B):
+        tiles = {}
+        direct = {}
+        for b in range(PE_FROM, B):
             for j in range(PACK):
-                rows.setdefault(max(-1, 3 * (b - 1) + LEAD[j]), []).append((b, j))
+                if j < PE_ROWS:
+                    tiles.setdefault(3 * (b - PE_FROM) + j + 1, []).append((b, j))
+                else:
+                    direct.setdefault(3 * (b - PE_FROM) + 1, []).append((b, j))
 
         square_row_on_vector(0, 0)
         for j in range(1, PACK):
             square_row(0, j)
         root(0)
-        for b, j in rows[-1]:
-            square_row(b, j)
+        for j in range(PACK):
+            square_row(1, j)
         root(1)
         for c in range(3):
             regroup_x(0, c)
         for c in range(3):
             quantise_x(0, c)
         weigh(0, 0, CH)
+        count = 0
         for u in range(UNITS + 1):
             b = u // 3
             c = u % 3
             if u < UNITS:
+                if c == 0 and b > 0:
+                    weigh(b, 0, D)
                 if b + 1 < B:
                     regroup_x(b + 1, c)
+            for bb, j in tiles.get(u - 1, []):
+                diagonal(bb, j)
+            if u < UNITS:
                 regroup_w(u)
                 if b + 1 < B:
                     quantise_x(b + 1, c)
                 if b == 0 and c < 2:
                     weigh(0, CH * (c + 1), CH * (c + 2))
-                if c == 2 and b + 1 < B:
-                    weigh(b + 1, 0, D)
             if u > 0:
                 for r in range(3):
                     if on_vector(u - 1, r):
                         leave(u - 1, r)
+            for bb, j in tiles.get(u + 1, []):
+                turn(count, bb, j)
+                count += 1
+            for bb, j in tiles.get(u, []):
+                turned_out(bb, j)
+                gram(bb, j)
             if u < UNITS:
                 quantise_w(u)
                 multiply(u)
-            ended = []
-            for bb, j in rows.get(u, []):
-                square_row(bb, j)
-                if j == PACK - 1:
-                    ended.append(bb)
             if u > 0:
                 for r in range(3):
                     if not on_vector(u - 1, r):
                         leave(u - 1, r)
-                        for bb in ended:
-                            root(bb)
-                        ended = []
+            for bb, j in direct.get(u, []):
+                square_row(bb, j)
+            for bb, j in tiles.get(u - 1, []):
+                if j == PE_ROWS - 1:
+                    root(bb)

@@ -44,7 +44,7 @@ def tile_globalmixture_kernel(tc, inputs, out):
         warm = keep.tile([P, 1], F32, name="warm")
         nc.scalar.activation(out=warm[:], in_=eps_t[:], func=ACT.Sqrt)
 
-        ident = keep.tile([P, P], F32, name="ident")
+        ident = keep.tile([P, P], BF16, name="ident")
         make_identity(nc, ident[:])
 
         xs = []
@@ -96,25 +96,22 @@ def tile_globalmixture_kernel(tc, inputs, out):
 
         def turn(n, b, j):
             sqt = psum.tile([P, WIDE], F32, name="sqt%d" % (n % 2))
-            words = xs[b][:, j, :].bitcast(F32)
-            for k in range(3):
-                nc.tensor.transpose(sqt[:, P * k : P * k + P], words[:, P * k : P * k + P], ident[:])
+            halves = sqt[:].bitcast(BF16)
+            for k in range(D // P):
+                nc.tensor.transpose(halves[:, P * k : P * k + P], xs[b][:, j, P * k : P * k + P], ident[:])
             turned[(b, j)] = sqt
 
         def turned_out(b, j):
-            xt = work.tile([P, WORDS], F32, name="xt")
-            nc.scalar.copy(out=xt[:], in_=turned[(b, j)][:, 0:WORDS])
+            xt = work.tile([P, D], BF16, name="xt")
+            nc.scalar.copy(out=xt[:].bitcast(F32), in_=turned[(b, j)][:, 0:WORDS])
             xts[(b, j)] = xt
 
         def gram(b, j):
-            halves = xts[(b, j)][:].bitcast(BF16)
-            for k in range(3):
-                for e in range(2):
-                    cols = halves[:, 2 * P * k + e : 2 * P * (k + 1) : 2]
-                    nc.tensor.matmul(
-                        turned[(b, j)][:, WORDS:WIDE], lhsT=cols, rhs=cols, start=(k == 0 and e == 0),
-                        stop=(k == 2 and e == 1),
-                    )
+            for k in range(D // P):
+                cols = xts[(b, j)][:, P * k : P * k + P]
+                nc.tensor.matmul(
+                    turned[(b, j)][:, WORDS:WIDE], lhsT=cols, rhs=cols, start=(k == 0), stop=(k == D // P - 1)
+                )
 
         def diagonal(b, j):
             ss = sums_of(b)

@@ -25,6 +25,8 @@ RUN = 4
 WORDS = D // 2
 PE_FROM = 2
 PE_ROWS = 3
+LATE = 1
+FINE = 18
 BANKS = 6
 
 
@@ -194,12 +196,14 @@ def tile_globalmixture_kernel(tc, inputs, out):
                 accs[(u, r)] = acc
 
         def on_vector(u, r):
+            if u % 6 == 4:
+                return r == 0
             return (r == 0 and u >= 3 * (B - 1)) or (r == 2 and u == UNITS - 1)
 
         def leave(u, r):
             if u not in results:
                 res = stage.tile([P, 2, D], F32, name="res")
-                results[u] = [res, 0]
+                results[u] = [res, set()]
             res = results[u][0]
             if r == 1:
                 part = (slice(0, 2), slice(WIDE, D))
@@ -211,13 +215,18 @@ def tile_globalmixture_kernel(tc, inputs, out):
                 nc.vector.tensor_copy(out=dst, in_=src)
             else:
                 nc.scalar.copy(out=dst, in_=src)
-            results[u][1] += 1
+            results[u][1].add(r)
             out_b = out[u // 3].rearrange("(m p) e -> p m e", p=P)
             m0 = 2 * (u % 3)
-            if u == UNITS - 1:
+            if u < FINE:
+                if len(results[u][1]) == 3:
+                    nc.sync.dma_start(out=out_b[:, m0 : m0 + 2, :], in_=res[:])
+            elif u < UNITS - 1:
+                for half in range(2):
+                    if r in (half, half + 1) and half in results[u][1] and half + 1 in results[u][1]:
+                        nc.sync.dma_start(out=out_b[:, m0 + half, :], in_=res[:, half, :])
+            else:
                 nc.sync.dma_start(out=out_b[:, m0 + part[0].start : m0 + part[0].stop, part[1]], in_=dst)
-            elif results[u][1] == 3:
-                nc.sync.dma_start(out=out_b[:, m0 : m0 + 2, :], in_=res[:])
 
         tiles = {}
         direct = {}
@@ -247,14 +256,14 @@ def tile_globalmixture_kernel(tc, inputs, out):
             if u < UNITS:
                 if c == 0 and b > 0:
                     weigh(b, 0, D)
-                if b + 1 < B:
-                    regroup_x(b + 1, c)
+                if u >= LATE and (u - LATE) // 3 + 1 < B:
+                    regroup_x((u - LATE) // 3 + 1, (u - LATE) % 3)
             for bb, j in tiles.get(u - 1, []):
                 diagonal(bb, j)
             if u < UNITS:
                 regroup_w(u)
-                if b + 1 < B:
-                    quantise_x(b + 1, c)
+                if u >= LATE and (u - LATE) // 3 + 1 < B:
+                    quantise_x((u - LATE) // 3 + 1, (u - LATE) % 3)
                 if b == 0 and c < 2:
                     weigh(0, CH * (c + 1), CH * (c + 2))
             if u > 0:

@@ -24,9 +24,10 @@ UNITS = 3 * B
 RUN = 4
 WORDS = D // 2
 PE_FROM = 2
-PE_ROWS = 3
+PE_ROWS = {2: 3, 3: 3, 4: 3, 5: 3, 6: 2, 7: 2}
+FAR = 2.0 ** 100
 LATE = 1
-FINE = 18
+FINE = 15
 BANKS = 6
 
 
@@ -48,6 +49,10 @@ def tile_globalmixture_kernel(tc, inputs, out):
 
         ident = keep.tile([P, P], BF16, name="ident")
         make_identity(nc, ident[:])
+        mask = keep.tile([P, P], BF16, name="mask")
+        nc.vector.tensor_scalar(
+            out=mask[:], in0=ident[:], scalar1=1.0, scalar2=FAR, op0=ALU.subtract, op1=ALU.mult
+        )
 
         xs = []
         for b in range(B):
@@ -70,6 +75,7 @@ def tile_globalmixture_kernel(tc, inputs, out):
         accs = {}
         turned = {}
         xts = {}
+        grams = {}
         results = {}
 
         def sums_of(b):
@@ -96,8 +102,8 @@ def tile_globalmixture_kernel(tc, inputs, out):
             nc.scalar.activation(out=w[:], in_=sums[b][:], func=ACT.Sqrt, bias=eps_t[:])
             norms[b] = w
 
-        def turn(n, b, j):
-            sqt = psum.tile([P, WIDE], F32, name="sqt%d" % (n % 2))
+        def turn(b, j):
+            sqt = psum.tile([P, WIDE], F32, name="sqt")
             halves = sqt[:].bitcast(BF16)
             for k in range(D // P):
                 nc.tensor.transpose(halves[:, P * k : P * k + P], xs[b][:, j, P * k : P * k + P], ident[:])
@@ -109,18 +115,17 @@ def tile_globalmixture_kernel(tc, inputs, out):
             xts[(b, j)] = xt
 
         def gram(b, j):
+            if b not in grams:
+                gr = psum.tile([P, PACK, P], F32, name="gr")
+                grams[b] = gr
+            nc.tensor.matmul(grams[b][:, j, :], lhsT=ident[:], rhs=mask[:], start=True, stop=False)
             for k in range(D // P):
                 cols = xts[(b, j)][:, P * k : P * k + P]
-                nc.tensor.matmul(
-                    turned[(b, j)][:, WORDS:WIDE], lhsT=cols, rhs=cols, start=(k == 0), stop=(k == D // P - 1)
-                )
+                nc.tensor.matmul(grams[b][:, j, :], lhsT=cols, rhs=cols, start=False, stop=(k == D // P - 1))
 
-        def diagonal(b, j):
-            ss = sums_of(b)
-            junk_d = work.tile([P, P], F32, name="junk_d")
-            nc.vector.scalar_tensor_tensor(
-                out=junk_d[:], in0=turned[(b, j)][:, WORDS:WIDE], scalar=1.0, in1=ident[:], op0=ALU.mult,
-                op1=ALU.mult, accum_out=ss[:, j : j + 1],
+        def diagonals(b):
+            nc.vector.tensor_reduce(
+                out=sums_of(b)[:, 0 : PE_ROWS[b]], in_=grams[b][:, 0 : PE_ROWS[b], :], op=ALU.max, axis=mybir.AxisListType.X
             )
 
         def regroup(dst, src):
@@ -196,7 +201,7 @@ def tile_globalmixture_kernel(tc, inputs, out):
                 accs[(u, r)] = acc
 
         def on_vector(u, r):
-            if u % 6 == 4:
+            if u % 9 == 4:
                 return r == 0
             return (r == 0 and u >= 3 * (B - 1)) or (r == 2 and u == UNITS - 1)
 
@@ -230,12 +235,15 @@ def tile_globalmixture_kernel(tc, inputs, out):
 
         tiles = {}
         direct = {}
+        ripe = {}
         for b in range(PE_FROM, B):
+            s = 3 * (b - PE_FROM)
             for j in range(PACK):
-                if j < PE_ROWS:
-                    tiles.setdefault(3 * (b - PE_FROM) + j + 1, []).append((b, j))
+                if j < PE_ROWS[b]:
+                    tiles.setdefault(s + j + 1, []).append((b, j))
                 else:
-                    direct.setdefault(3 * (b - PE_FROM) + 1, []).append((b, j))
+                    direct.setdefault(s + 2, []).append((b, j))
+            ripe.setdefault(s + PE_ROWS[b] + 1, []).append(b)
 
         square_row_on_vector(0, 0)
         for j in range(1, PACK):
@@ -249,32 +257,33 @@ def tile_globalmixture_kernel(tc, inputs, out):
         for c in range(3):
             quantise_x(0, c)
         weigh(0, 0, CH)
-        count = 0
+        for bb, j in tiles.get(0, []):
+            turn(bb, j)
         for u in range(UNITS + 1):
             b = u // 3
             c = u % 3
+            late = u - LATE
             if u < UNITS:
                 if c == 0 and b > 0:
                     weigh(b, 0, D)
-                if u >= LATE and (u - LATE) // 3 + 1 < B:
-                    regroup_x((u - LATE) // 3 + 1, (u - LATE) % 3)
-            for bb, j in tiles.get(u - 1, []):
-                diagonal(bb, j)
-            if u < UNITS:
+                if late >= 0 and late // 3 + 1 < B:
+                    regroup_x(late // 3 + 1, late % 3)
                 regroup_w(u)
-                if u >= LATE and (u - LATE) // 3 + 1 < B:
-                    quantise_x((u - LATE) // 3 + 1, (u - LATE) % 3)
+                if late >= 0 and late // 3 + 1 < B:
+                    quantise_x(late // 3 + 1, late % 3)
                 if b == 0 and c < 2:
                     weigh(0, CH * (c + 1), CH * (c + 2))
+            for bb in ripe.get(u, []):
+                diagonals(bb)
             if u > 0:
                 for r in range(3):
                     if on_vector(u - 1, r):
                         leave(u - 1, r)
-            for bb, j in tiles.get(u + 1, []):
-                turn(count, bb, j)
-                count += 1
             for bb, j in tiles.get(u, []):
                 turned_out(bb, j)
+            for bb, j in tiles.get(u + 1, []):
+                turn(bb, j)
+            for bb, j in tiles.get(u, []):
                 gram(bb, j)
             if u < UNITS:
                 quantise_w(u)
@@ -285,6 +294,7 @@ def tile_globalmixture_kernel(tc, inputs, out):
                         leave(u - 1, r)
             for bb, j in direct.get(u, []):
                 square_row(bb, j)
-            for bb, j in tiles.get(u - 1, []):
-                if j == PE_ROWS - 1:
+            for bb in range(PE_FROM, B):
+                s = 3 * (bb - PE_FROM)
+                if u == max(s + 2, s + PE_ROWS[bb] + 1):
                     root(bb)

@@ -201,7 +201,7 @@ def tile_globalmixture_kernel(tc, inputs, out):
                 accs[(u, r)] = acc
 
         def on_vector(u, r):
-            if u % 9 == 4:
+            if u == 13:
                 return r == 0
             return (r == 0 and u >= 3 * (B - 1)) or (r == 2 and u == UNITS - 1)
 
@@ -238,25 +238,26 @@ def tile_globalmixture_kernel(tc, inputs, out):
         ripe = {}
         for b in range(PE_FROM, B):
             s = 3 * (b - PE_FROM)
+            first = s + 2 if b == 6 else s + 1
             for j in range(PACK):
                 if j < PE_ROWS[b]:
-                    tiles.setdefault(s + j + 1, []).append((b, j))
+                    tiles.setdefault(first + j, []).append((b, j))
                 else:
                     direct.setdefault(s + 2, []).append((b, j))
-            ripe.setdefault(s + PE_ROWS[b] + 1, []).append(b)
+            ripe.setdefault(first + PE_ROWS[b], []).append(b)
 
-        square_row_on_vector(0, 0)
-        for j in range(1, PACK):
+        square_row_on_vector(0, 1)
+        for j in (0, 2, 3):
             square_row(0, j)
         root(0)
         for j in range(PACK):
             square_row(1, j)
-        root(1)
         for c in range(3):
             regroup_x(0, c)
-        for c in range(3):
-            quantise_x(0, c)
+        quantise_x(0, 0)
+        quantise_x(0, 1)
         weigh(0, 0, CH)
+        quantise_x(0, 2)
         for bb, j in tiles.get(0, []):
             turn(bb, j)
         for u in range(UNITS + 1):
@@ -292,9 +293,9 @@ def tile_globalmixture_kernel(tc, inputs, out):
                 for r in range(3):
                     if not on_vector(u - 1, r):
                         leave(u - 1, r)
+                    if u == 1 and r == 0:
+                        root(1)
             for bb, j in direct.get(u, []):
                 square_row(bb, j)
-            for bb in range(PE_FROM, B):
-                s = 3 * (bb - PE_FROM)
-                if u == max(s + 2, s + PE_ROWS[bb] + 1):
-                    root(bb)
+            for bb in ripe.get(u, []):
+                root(bb)

from contextlib import ExitStack

import concourse.mybir as mybir
from concourse.masks import make_identity

FLOPS = 2 * 8 * 512 * 768 * 768

BF16 = mybir.dt.bfloat16
F32 = mybir.dt.float32
U32 = mybir.dt.uint32
U8 = mybir.dt.uint8
FP8X4 = mybir.dt.float8_e4m3fn_x4
ACT = mybir.ActivationFunctionType
ALU = mybir.AluOpType

B = 8
D = 768
P = 128
PACK = 4
EPS = 1e-05
WIDE = 512
CH = 256
UNITS = 3 * B
RUN = 4
WORDS = D // 2
PE_FROM = 2
PE_ROWS = {2: 3, 3: 3, 4: 3, 5: 3, 6: 2, 7: 2}
FAR = 2.0 ** 100
LATE = 1
FINE = 15
BANKS = 6


def tile_globalmixture_kernel(tc, inputs, out):
    nc = tc.nc
    with ExitStack() as ctx:
        keep = ctx.enter_context(tc.tile_pool(name="keep", bufs=1))
        small = ctx.enter_context(tc.tile_pool(name="small", bufs=4))
        work = ctx.enter_context(tc.tile_pool(name="work", bufs=3))
        quant = ctx.enter_context(tc.tile_pool(name="quant", bufs=4))
        stage = ctx.enter_context(tc.tile_pool(name="stage", bufs=8))
        psum = ctx.enter_context(tc.psum_pool(name="psum", bufs=1))
        ctx.enter_context(tc.manual_schedule())

        eps_t = keep.tile([P, 1], F32, name="eps_t")
        nc.vector.memset(eps_t[:], EPS)
        warm = keep.tile([P, 1], F32, name="warm")
        nc.scalar.activation(out=warm[:], in_=eps_t[:], func=ACT.Sqrt)

        ident = keep.tile([P, P], BF16, name="ident")
        make_identity(nc, ident[:])
        mask = keep.tile([P, P], BF16, name="mask")
        nc.vector.tensor_scalar(
            out=mask[:], in0=ident[:], scalar1=1.0, scalar2=FAR, op0=ALU.subtract, op1=ALU.mult
        )

        xs = []
        for b in range(B):
            xt = keep.tile([P, PACK, D], BF16, name="x%d" % b)
            src = inputs[b].rearrange("(p j) d -> p j d", j=PACK)
            if b == 0:
                for j in range(PACK):
                    nc.sync.dma_start(out=xt[:, j, :], in_=src[:, j, :])
            else:
                nc.sync.dma_start(out=xt[:], in_=src)
            xs.append(xt)

        sums = {}
        norms = {}
        xgs = {}
        xops = {}
        xwns = {}
        wgs = {}
        wops = {}
        accs = {}
        turned = {}
        xts = {}
        grams = {}
        results = {}

        def sums_of(b):
            if b not in sums:
                ss = small.tile([P, PACK], F32, name="ss")
                sums[b] = ss
            return sums[b]

        def square_row(b, j):
            ss = sums_of(b)
            junk_s = work.tile([P, D], BF16, name="junk_s")
            nc.scalar.activation(out=junk_s[:], in_=xs[b][:, j, :], func=ACT.Square, accum_out=ss[:, j : j + 1])

        def square_row_on_vector(b, j):
            ss = sums_of(b)
            junk_v = work.tile([P, D], BF16, name="junk_v")
            nc.vector.scalar_tensor_tensor(
                out=junk_v[:], in0=xs[b][:, j, :], scalar=1.0, in1=xs[b][:, j, :], op0=ALU.mult, op1=ALU.mult,
                accum_out=ss[:, j : j + 1],
            )

        def root(b):
            w = small.tile([P, PACK], F32, name="w")
            nc.scalar.activation(out=w[:], in_=sums[b][:], func=ACT.Sqrt, bias=eps_t[:])
            norms[b] = w

        def turn(b, j):
            sqt = psum.tile([P, WIDE], F32, name="sqt")
            halves = sqt[:].bitcast(BF16)
            for k in range(D // P):
                nc.tensor.transpose(halves[:, P * k : P * k + P], xs[b][:, j, P * k : P * k + P], ident[:])
            turned[(b, j)] = sqt

        def turned_out(b, j):
            xt = work.tile([P, D], BF16, name="xt")
            nc.scalar.copy(out=xt[:].bitcast(F32), in_=turned[(b, j)][:, 0:WORDS])
            xts[(b, j)] = xt

        def gram(b, j):
            if b not in grams:
                gr = psum.tile([P, PACK, P], F32, name="gr")
                grams[b] = gr
            nc.tensor.matmul(grams[b][:, j, :], lhsT=ident[:], rhs=mask[:], start=True, stop=False)
            for k in range(D // P):
                cols = xts[(b, j)][:, P * k : P * k + P]
                nc.tensor.matmul(grams[b][:, j, :], lhsT=cols, rhs=cols, start=False, stop=(k == D // P - 1))

        def diagonals(b):
            nc.vector.tensor_reduce(
                out=sums_of(b)[:, 0 : PE_ROWS[b]], in_=grams[b][:, 0 : PE_ROWS[b], :], op=ALU.max, axis=mybir.AxisListType.X
            )

        def regroup(dst, src):
            nc.vector.tensor_copy(
                out=dst.rearrange("p (c i) t -> p c t i", i=RUN),
                in_=src.rearrange("p t (c i) -> p c t i", i=RUN),
            )

        def regroup_x(b, c):
            xg = work.tile([P, CH, PACK], BF16, name="xg", align_bytes=64)
            regroup(xg[:], xs[b][:, :, CH * c : CH * c + CH])
            xgs[(b, c)] = xg

        def quantise_x(b, c):
            if b not in xops:
                xc = quant.tile([P, D], U32, name="xc", align_bytes=64)
                xsc = quant.tile([P, D], U8, name="xsc", align_bytes=64)
                xops[b] = (xc, xsc)
            xc, xsc = xops[b]
            nc.vector.quantize_mx(
                out=xc[:, CH * c : CH * c + CH].bitcast(FP8X4),
                scales=xsc[:, CH * c : CH * c + CH],
                in_=xgs[(b, c)][:].rearrange("p w j -> p (w j)"),
            )

        def weigh(b, lo, hi):
            if b not in xwns:
                xwn = work.tile([P, PACK, D], BF16, name="xwn")
                xwns[b] = xwn
            for j in range(PACK):
                nc.vector.tensor_scalar(
                    out=xwns[b][:, j, lo:hi], in0=xs[b][:, j, lo:hi], scalar1=norms[b][:, j : j + 1],
                    scalar2=None, op0=ALU.mult,
                )

        def regroup_w(u):
            c = u % 3
            xwg = work.tile([P, CH, PACK], BF16, name="xwg", align_bytes=64)
            regroup(xwg[:], xwns[u // 3][:, :, CH * c : CH * c + CH])
            wgs[u] = xwg

        def quantise_w(u):
            wc = quant.tile([P, CH], U32, name="wc", align_bytes=64)
            wsc = quant.tile([P, CH], U8, name="wsc", align_bytes=64)
            nc.vector.quantize_mx(
                out=wc[:].bitcast(FP8X4), scales=wsc[:], in_=wgs[u][:].rearrange("p w j -> p (w j)")
            )
            wops[u] = (wc, wsc)

        def mx(acc, u, half, lo, hi):
            xc, xsc = xops[u // 3]
            wc, wsc = wops[u]
            nc.tensor.matmul_mx(
                out=acc,
                lhsT=wc[:, P * half : P * half + P].bitcast(FP8X4),
                lhsT_scale=wsc[:, P * half : P * half + P],
                rhs=xc[:, lo:hi].bitcast(FP8X4),
                rhs_scale=xsc[:, lo:hi],
                start=True,
                stop=True,
            )

        def multiply(u):
            for r in range(3):
                slot = (3 * u + r) % BANKS
                if r == 1:
                    acc = psum.tile([P, 2, CH], F32, name="acc%d" % slot)
                    mx(acc[:, 0, :], u, 0, WIDE, D)
                    mx(acc[:, 1, :], u, 1, WIDE, D)
                else:
                    acc = psum.tile([P, WIDE], F32, name="acc%d" % slot)
                    mx(acc[:], u, r // 2, 0, WIDE)
                accs[(u, r)] = acc

        def on_vector(u, r):
            if u == 13:
                return r == 0
            return (r == 0 and u >= 3 * (B - 1)) or (r == 2 and u == UNITS - 1)

        def leave(u, r):
            if u not in results:
                res = stage.tile([P, 2, D], F32, name="res")
                results[u] = [res, set()]
            res = results[u][0]
            if r == 1:
                part = (slice(0, 2), slice(WIDE, D))
            else:
                part = (slice(r // 2, r // 2 + 1), slice(0, WIDE))
            dst = res[:, part[0], part[1]]
            src = accs[(u, r)][:] if r == 1 else accs[(u, r)][:].unsqueeze(1)
            if on_vector(u, r):
                nc.vector.tensor_copy(out=dst, in_=src)
            else:
                nc.scalar.copy(out=dst, in_=src)
            results[u][1].add(r)
            out_b = out[u // 3].rearrange("(m p) e -> p m e", p=P)
            m0 = 2 * (u % 3)
            if u < FINE:
                if len(results[u][1]) == 3:
                    nc.sync.dma_start(out=out_b[:, m0 : m0 + 2, :], in_=res[:])
            elif u < UNITS - 1:
                for half in range(2):
                    if r in (half, half + 1) and half in results[u][1] and half + 1 in results[u][1]:
                        nc.sync.dma_start(out=out_b[:, m0 + half, :], in_=res[:, half, :])
            else:
                nc.sync.dma_start(out=out_b[:, m0 + part[0].start : m0 + part[0].stop, part[1]], in_=dst)

        tiles = {}
        direct = {}
        ripe = {}
        for b in range(PE_FROM, B):
            s = 3 * (b - PE_FROM)
            first = s + 2 if b == 6 else s + 1
            for j in range(PACK):
                if j < PE_ROWS[b]:
                    tiles.setdefault(first + j, []).append((b, j))
                else:
                    direct.setdefault(s + 2, []).append((b, j))
            ripe.setdefault(first + PE_ROWS[b], []).append(b)

        square_row_on_vector(0, 1)
        for j in (0, 2, 3):
            square_row(0, j)
        root(0)
        for j in range(PACK):
            square_row(1, j)
        for c in range(3):
            regroup_x(0, c)
        quantise_x(0, 0)
        quantise_x(0, 1)
        weigh(0, 0, CH)
        quantise_x(0, 2)
        for bb, j in tiles.get(0, []):
            turn(bb, j)
        for u in range(UNITS + 1):
            b = u // 3
            c = u % 3
            late = u - LATE
            if u < UNITS:
                if c == 0 and b > 0:
                    weigh(b, 0, D)
                if late >= 0 and late // 3 + 1 < B:
                    regroup_x(late // 3 + 1, late % 3)
                regroup_w(u)
                if late >= 0 and late // 3 + 1 < B:
                    quantise_x(late // 3 + 1, late % 3)
                if b == 0 and c < 2:
                    weigh(0, CH * (c + 1), CH * (c + 2))
            for bb in ripe.get(u, []):
                diagonals(bb)
            if u > 0:
                for r in range(3):
                    if on_vector(u - 1, r):
                        leave(u - 1, r)
            for bb, j in tiles.get(u, []):
                turned_out(bb, j)
            for bb, j in tiles.get(u + 1, []):
                turn(bb, j)
            for bb, j in tiles.get(u, []):
                gram(bb, j)
            if u < UNITS:
                quantise_w(u)
                multiply(u)
            if u > 0:
                for r in range(3):
                    if not on_vector(u - 1, r):
                        leave(u - 1, r)
                    if u == 1 and r == 0:
                        root(1)
            for bb, j in direct.get(u, []):
                square_row(bb, j)
            for bb in ripe.get(u, []):
                root(bb)
